import numpy as np
import ml_dtypes


def mxq(x, axis, fmt="e4m3"):
    dtype, down = {"e4m3": (ml_dtypes.float8_e4m3fn, 7), "e5m2": (ml_dtypes.float8_e5m2, 14)}[fmt]
    v = np.moveaxis(np.asarray(x, np.float32).astype(ml_dtypes.bfloat16).astype(np.float64), axis, -1)
    blocks = v.reshape(v.shape[:-1] + (-1, 32))
    amax = np.abs(blocks).max(-1, keepdims=True)
    byte = np.maximum(np.where(amax > 0, np.frexp(amax)[1] - 1 + 127, 0) - down, 1)
    scale = np.exp2(byte - 127.0)
    codes = (blocks / scale).astype(np.float32).astype(dtype).astype(np.float64)
    return np.moveaxis((codes * scale).reshape(v.shape), -1, axis)


WIDE = False


def mx_kscale(k):
    if not WIDE:
        return np.ones(k)
    levels = np.array([10, -10, 5, -5, 0])
    a = np.random.permutation(np.resize(levels, k // 512 * 4)).reshape(k // 512, 4)
    idx = np.arange(k)
    return np.exp2(a[idx // 512, idx % 128 // 32])


BF16 = ml_dtypes.bfloat16


def bf(x):
    return np.asarray(x, np.float32).astype(BF16)


def f64(x):
    return np.asarray(x).astype(np.float64)


B, N, DIM, H, DH = 2, 256, 1536, 16, 96
D1 = DH // 3


def rotate_half(t):
    d = t.shape[-1]
    t1, t2 = t[..., : (d + 1) // 2], t[..., (d + 1) // 2:]
    return np.concatenate((-t2, t1), axis=-1)


def apply_rope(t, freqs):
    return t * np.cos(freqs) + rotate_half(t) * np.sin(freqs)


def rope3(t, fs):
    return np.concatenate([apply_rope(ts, f) for ts, f in zip(np.split(t, (D1, 2 * D1), axis=-1), fs)], axis=-1)


def setup_inputs():
    s = mx_kscale(DIM)
    return {"x": bf(np.random.standard_normal((B, N, DIM)) * s),
            "f1": bf(np.random.uniform(0.0, 1.0, (N, D1))),
            "f2": bf(np.random.uniform(0.0, 1.0, (N, D1))),
            "f3": bf(np.random.uniform(0.0, 1.0, (N, D1))),
            "Wqkv": bf(np.random.standard_normal((DIM, 3 * H * DH)) / np.sqrt(DIM) / s[:, None])}


def reference(x, f1, f2, f3, Wqkv):
    qkv = mxq(f64(x), 2, "e4m3") @ mxq(f64(Wqkv), 0, "e4m3")
    q, k, v = np.split(qkv, 3, axis=-1)
    to_heads = lambda t: t.reshape(B, N, H, DH).transpose(0, 2, 1, 3)
    q, k, v = to_heads(q), to_heads(k), to_heads(v)
    fs = (f64(f1), f64(f2), f64(f3))
    return rope3(q, fs), rope3(k, fs), v

@@ -1,0 +1,309 @@
+import math
+from contextlib import ExitStack
+
+import concourse.mybir as mybir
+from concourse.masks import make_identity
+
+F32 = mybir.dt.float32
+BF16 = mybir.dt.bfloat16
+U32 = mybir.dt.uint32
+U8 = mybir.dt.uint8
+FP8X4 = mybir.dt.float8_e4m3fn_x4
+MULT = mybir.AluOpType.mult
+ADD = mybir.AluOpType.add
+SIN = mybir.ActivationFunctionType.Sin
+
+BATCH, TOKENS, DIM, HEADS, HEAD_DIM = 2, 256, 1536, 16, 96
+SECTIONS = 3
+ROPE_SECTIONS = 2
+AXES, HALF = 3, 16
+
+P = 128
+PACK = 4
+K_PASS = P * PACK
+PASSES = DIM // K_PASS
+PAIR = TOKENS // P
+
+UNIT_HEADS = 4
+UNIT = UNIT_HEADS * HEAD_DIM
+WIDE = 256
+UNITS_PER_SECTION = HEADS // UNIT_HEADS
+UNITS = SECTIONS * UNITS_PER_SECTION
+LOAD_UNITS = 2
+LOAD_COLS = LOAD_UNITS * UNIT
+LOADS = UNITS // LOAD_UNITS
+AHEAD = 2
+BANK = 512
+
+FLOPS = 2 * BATCH * TOKENS * DIM * SECTIONS * HEADS * HEAD_DIM
+
+
+def tile_attention_pa_kernel(tc, x, f1, f2, f3, Wqkv, out_0, out_1, out_2):
+    nc = tc.nc
+    outs = (out_0, out_1, out_2)
+
+    with ExitStack() as ctx:
+        const = ctx.enter_context(tc.tile_pool(name="const", bufs=1))
+        single = ctx.enter_context(tc.tile_pool(name="single", bufs=2))
+        double = ctx.enter_context(tc.tile_pool(name="double", bufs=1))
+        fetched = ctx.enter_context(tc.tile_pool(name="fetched", bufs=2))
+        stage = ctx.enter_context(tc.tile_pool(name="stage", bufs=3))
+        packed = ctx.enter_context(tc.tile_pool(name="packed", bufs=4))
+        result = ctx.enter_context(tc.tile_pool(name="result", bufs=4))
+        psum = ctx.enter_context(tc.psum_pool(name="psum", bufs=8))
+
+        order = list(range(UNITS))
+
+        def rotated(unit):
+            return unit // UNITS_PER_SECTION < ROPE_SECTIONS
+
+        x_sb = [
+            result.tile([P, PAIR * DIM], BF16, align_bytes=64, name="scaled") for c in range(2)
+        ]
+        raw_of = {}
+
+        def load_x(c):
+            for b in range(BATCH):
+                nc.sync.dma_start(
+                    out=x_sb[c][b:P:BATCH, :],
+                    in_=x[b].rearrange("(m c f) k -> m c (f k)", c=2, f=PAIR)[:, c, :],
+                )
+
+        pool_of = {1: single, 2: double, 4: fetched}
+
+        def load_weights(units):
+            cols = len(units) * UNIT
+            col0 = units[0] * UNIT
+            w_raw = pool_of[len(units)].tile([P, PASSES, PACK, cols], BF16, name="w_raw")
+            for g in range(PASSES):
+                nc.sync.dma_start(
+                    out=w_raw[:, g, :, :],
+                    in_=Wqkv[g * K_PASS : (g + 1) * K_PASS, col0 : col0 + cols].rearrange(
+                        "(p j) w -> p j w", j=PACK
+                    ),
+                )
+            for i, unit in enumerate(units):
+                raw_of[unit] = (w_raw, i * UNIT)
+
+        angles = const.tile([P, AXES, BATCH * PAIR, 2 * HALF], BF16)
+
+        load_weights([0])
+        load_x(0)
+        load_x(1)
+        load_weights([1])
+        for axis, f in enumerate((f1, f2, f3)):
+            for b in range(BATCH):
+                nc.sync.dma_start(
+                    out=angles[b:P:BATCH, axis].rearrange("p t c -> p (t c)"),
+                    in_=f.rearrange("(m t) c -> m (t c)", t=BATCH * PAIR),
+                )
+        load_weights([2, 3])
+        load_weights([4, 5, 6, 7])
+
+        factors = const.tile([P, BATCH, PAIR, 2, AXES, 2, HALF], F32)
+        warm = const.tile([P, 2], F32)
+        nc.gpsimd.memset(warm[:, 0:1], 0.0)
+
+        def make_factors():
+            by_token = factors[:].rearrange("p c e z a s i -> p (c e) z a s i")
+            halves = angles[:].rearrange("p a t (s i) -> p t a s i", s=2)
+            nc.scalar.activation(
+                out=by_token[:, :, 0].rearrange("p t a s i -> p t a (s i)"),
+                in_=angles[:].rearrange("p a t c -> p t a c"),
+                func=SIN,
+                scale=-1.0,
+                bias=math.pi / 2,
+            )
+            nc.scalar.activation(out=by_token[:, :, 1, :, 0, :], in_=halves[:, :, :, 1, :], func=SIN)
+            nc.scalar.activation(
+                out=by_token[:, :, 1, :, 1, :], in_=halves[:, :, :, 0, :], func=SIN, scale=-1.0
+            )
+
+        ident = const.tile([P, P], F32)
+        make_identity(nc, ident[:])
+        x_words = [
+            x_sb[c][:].bitcast(F32).rearrange("p (e g q u) -> p e g u q", e=PAIR, g=PASSES, u=2)
+            for c in range(2)
+        ]
+        x_grouped = result.tile(
+            [P, PASSES * BATCH * PAIR * P * PACK], BF16, align_bytes=64, name="scaled"
+        )
+        x_grouped_words = x_grouped[:].bitcast(F32).rearrange(
+            "p (g b e t u) -> p g b e t u", g=PASSES, b=BATCH, e=PAIR, u=2
+        )
+        x_grouped_cols = x_grouped[:].rearrange("p (g b c) -> p g b c", g=PASSES, b=BATCH)
+        x_codes = const.tile([P, PASSES, BATCH, PAIR * P], U32, align_bytes=64)
+        x_scales = const.tile([P, PASSES, BATCH, PAIR * P], U8, align_bytes=64)
+
+        def turn_x(b):
+            for g in range(PASSES):
+                turned = psum.tile([P, BANK], F32, name="bank")
+                turned_words = turned[:].rearrange("p (e u t) -> p e u t", e=PAIR, u=2)
+                for e in range(PAIR):
+                    for u in range(2):
+                        nc.tensor.transpose(
+                            turned_words[:, e, u, :], x_words[b][:, e, g, u, :], ident[:]
+                        )
+                nc.scalar.copy(
+                    out=x_grouped_words[:, g, b],
+                    in_=turned_words.rearrange("p e u t -> p e t u"),
+                )
+
+        def quantise_x(b):
+            for g in range(PASSES):
+                nc.vector.quantize_mx(
+                    out=x_codes[:, g, b, :].bitcast(FP8X4),
+                    scales=x_scales[:, g, b, :],
+                    in_=x_grouped_cols[:, g, b, :],
+                )
+
+        grouped_of = {}
+        packed_of = {}
+
+        def regroup(n, vector_passes):
+            raw, col0 = raw_of[order[n]]
+            grouped = stage.tile([P, PASSES, UNIT, PACK], BF16, align_bytes=64, name="grouped")
+            grouped_of[n] = grouped
+            for g in range(PASSES):
+                src = raw[:, g, :, col0 : col0 + UNIT].rearrange("p j (c i) -> p c j i", i=4)
+                dst = grouped[:, g, :, :].rearrange("p (c i) j -> p c j i", i=4)
+                if g in vector_passes:
+                    nc.vector.tensor_copy(out=dst, in_=src)
+                else:
+                    nc.scalar.copy(out=dst, in_=src)
+
+        def quantise(n):
+            codes = packed.tile([P, PASSES * UNIT], U32, align_bytes=64, name="codes")
+            scales = packed.tile([P, PASSES * UNIT], U8, align_bytes=64, name="scales")
+            packed_of[n] = (codes, scales)
+            flat = grouped_of[n][:].rearrange("p g w j -> p (g w j)")
+            for part in (slice(0, 1024), slice(1024, PASSES * UNIT)):
+                nc.vector.quantize_mx(
+                    out=codes[:, part].bitcast(FP8X4),
+                    scales=scales[:, part],
+                    in_=flat[:, PACK * part.start : PACK * part.stop],
+                )
+
+        banks_of = {}
+
+        def multiply(n, b):
+            codes, scales = packed_of[n]
+            for e in range(PAIR):
+                bank = psum.tile([P, BANK], F32, name="bank")
+                tokens = slice(e * P, (e + 1) * P)
+                for part in (slice(0, WIDE), slice(WIDE, UNIT)):
+                    for g in range(PASSES):
+                        cols = slice(g * UNIT + part.start, g * UNIT + part.stop)
+                        nc.tensor.matmul_mx(
+                            out=bank[:, part],
+                            lhsT=x_codes[:, g, b, tokens].bitcast(FP8X4),
+                            lhsT_scale=x_scales[:, g, b, tokens],
+                            rhs=codes[:, cols].bitcast(FP8X4),
+                            rhs_scale=scales[:, cols],
+                            start=(g == 0),
+                            stop=(g == PASSES - 1),
+                        )
+                banks_of[(n, b, e)] = bank[:, 0:UNIT].rearrange("p (h d) -> p h d", h=UNIT_HEADS)
+
+        shape = [P, 2, UNIT_HEADS, HEAD_DIM]
+
+        def products(n, scaled):
+            for b in range(BATCH):
+                for e in range(PAIR):
+                    nc.vector.tensor_tensor(
+                        out=scaled[:, :, :, b, e, :],
+                        in0=banks_of[(n, b, e)].unsqueeze(1).to_broadcast(shape),
+                        in1=factors[:, b, e]
+                        .rearrange("p z a s i -> p z (a s i)")
+                        .unsqueeze(2)
+                        .to_broadcast(shape),
+                        op=MULT,
+                    )
+
+        def sums(engine, scaled, s, rows):
+            halves = scaled[:].rearrange("p z h c e (a s i) -> p z (h c e) a s i", a=AXES, s=2)
+            engine.tensor_tensor(
+                out=halves[:, 0, rows, :, s, :],
+                in0=halves[:, 0, rows, :, s, :],
+                in1=halves[:, 1, rows, :, 1 - s, :],
+                op=ADD,
+            )
+
+        def store(n, scaled, b):
+            unit = order[n]
+            head = (unit % UNITS_PER_SECTION) * UNIT_HEADS
+            nc.sync.dma_start(
+                out=outs[unit // UNITS_PER_SECTION][b, head : head + UNIT_HEADS].rearrange(
+                    "h (m t) d -> m h (t d)", t=BATCH * PAIR
+                ),
+                in_=scaled[b:P:BATCH, 0].rearrange("p h c e d -> p h (c e d)"),
+            )
+
+        def store_half(n, scaled, b, c):
+            unit = order[n]
+            head = (unit % UNITS_PER_SECTION) * UNIT_HEADS
+            nc.sync.dma_start(
+                out=outs[unit // UNITS_PER_SECTION][b, head : head + UNIT_HEADS].rearrange(
+                    "h (m c f) d -> m h c (f d)", c=2, f=PAIR
+                )[:, :, c, :],
+                in_=scaled[b:P:BATCH, 0, :, c].rearrange("p h e d -> p h (e d)"),
+            )
+
+        ROWS = BATCH * UNIT_HEADS * PAIR
+        every = slice(0, ROWS)
+        lower = slice(0, ROWS // 2)
+        upper = slice(ROWS // 2, ROWS)
+        fence = const.tile([P, 1], U32)
+
+        with tc.manual_schedule():
+            nc.scalar.activation(out=warm[:, 1:2], in_=warm[:, 0:1], func=SIN)
+            pending = []
+            for n in range(-2, UNITS):
+                if n == -1:
+                    turn_x(0)
+                    quantise_x(0)
+                    turn_x(1)
+                    quantise_x(1)
+                if 0 <= n + 1 < UNITS:
+                    quantise(n + 1)
+                    for b in range(BATCH):
+                        multiply(n + 1, b)
+                if n >= 0 and rotated(order[n]):
+                    scaled = result.tile(
+                        [P, 2, UNIT_HEADS, BATCH, PAIR, HEAD_DIM], F32, align_bytes=64, name="scaled"
+                    )
+                    if pending:
+                        if n + 1 < UNITS:
+                            nc.gpsimd.tensor_copy(out=fence[:], in_=packed_of[n + 1][0][:, 1024:1025])
+                        sums(nc.gpsimd, pending[1], 0, every)
+                        sums(nc.gpsimd, pending[1], 1, lower)
+                    products(n, scaled)
+                    if pending:
+                        sums(nc.vector, pending[1], 1, upper)
+                        for b in range(BATCH):
+                            store(pending[0], pending[1], b)
+                    pending = [n, scaled]
+                elif n >= 0:
+                    scaled = result.tile(
+                        [P, 1, UNIT_HEADS, BATCH, PAIR, HEAD_DIM], F32, align_bytes=64, name="scaled"
+                    )
+                    for c in range(2):
+                        for e in range(PAIR):
+                            nc.scalar.copy(out=scaled[:, 0, :, c, e, :], in_=banks_of[(n, c, e)])
+                        if n == UNITS - 1:
+                            for b in range(BATCH):
+                                store_half(n, scaled, b, c)
+                    if n < UNITS - 1:
+                        for b in range(BATCH):
+                            store(n, scaled, b)
+                if n == 2:
+                    load_weights([8, 9, 10, 11])
+                if n + 2 < UNITS:
+                    regroup(n + 2, (1, 2) if n < 0 or not rotated(order[n]) else ())
+                if n == -1:
+                    make_factors()
+                if n == ROPE_SECTIONS * UNITS_PER_SECTION - 1:
+                    for s in range(2):
+                        sums(nc.vector, pending[1], s, every)
+                    for b in range(BATCH):
+                        store(pending[0], pending[1], b)

@@ -29,10 +29,9 @@ UNIT = UNIT_HEADS * HEAD_DIM
 WIDE = 256
 UNITS_PER_SECTION = HEADS // UNIT_HEADS
 UNITS = SECTIONS * UNITS_PER_SECTION
-LOAD_UNITS = 2
-LOAD_COLS = LOAD_UNITS * UNIT
-LOADS = UNITS // LOAD_UNITS
-AHEAD = 2
+PIECES = ((0,), (1,), (2,), (3, 4), (5, 6, 7), (8, 9, 10, 11))
+V_TURN = 3
+EARLY = 4
 BANK = 512
 
 FLOPS = 2 * BATCH * TOKENS * DIM * SECTIONS * HEADS * HEAD_DIM
@@ -44,9 +43,7 @@ def tile_attention_pa_kernel(tc, x, f1, f2, f3, Wqkv, out_0, out_1, out_2):
 
     with ExitStack() as ctx:
         const = ctx.enter_context(tc.tile_pool(name="const", bufs=1))
-        single = ctx.enter_context(tc.tile_pool(name="single", bufs=2))
-        double = ctx.enter_context(tc.tile_pool(name="double", bufs=1))
-        fetched = ctx.enter_context(tc.tile_pool(name="fetched", bufs=2))
+        fetched = ctx.enter_context(tc.tile_pool(name="fetched", bufs=1))
         stage = ctx.enter_context(tc.tile_pool(name="stage", bufs=3))
         packed = ctx.enter_context(tc.tile_pool(name="packed", bufs=4))
         result = ctx.enter_context(tc.tile_pool(name="result", bufs=4))
@@ -69,12 +66,10 @@ def tile_attention_pa_kernel(tc, x, f1, f2, f3, Wqkv, out_0, out_1, out_2):
                     in_=x[b].rearrange("(m c f) k -> m c (f k)", c=2, f=PAIR)[:, c, :],
                 )
 
-        pool_of = {1: single, 2: double, 4: fetched}
-
-        def load_weights(units):
-            cols = len(units) * UNIT
-            col0 = units[0] * UNIT
-            w_raw = pool_of[len(units)].tile([P, PASSES, PACK, cols], BF16, name="w_raw")
+        def load_weights(piece):
+            cols = len(PIECES[piece]) * UNIT
+            col0 = PIECES[piece][0] * UNIT
+            w_raw = fetched.tile([P, PASSES, PACK, cols], BF16, name="w_raw%d" % piece)
             for g in range(PASSES):
                 nc.sync.dma_start(
                     out=w_raw[:, g, :, :],
@@ -82,27 +77,28 @@ def tile_attention_pa_kernel(tc, x, f1, f2, f3, Wqkv, out_0, out_1, out_2):
                         "(p j) w -> p j w", j=PACK
                     ),
                 )
-            for i, unit in enumerate(units):
+            for i, unit in enumerate(PIECES[piece]):
                 raw_of[unit] = (w_raw, i * UNIT)
 
         angles = const.tile([P, AXES, BATCH * PAIR, 2 * HALF], BF16)
+        warm = const.tile([P, 2], F32)
+        nc.gpsimd.memset(warm[:, 0:1], 0.0)
+        ident = const.tile([P, P], F32)
+        make_identity(nc, ident[:])
 
-        load_weights([0])
-        load_x(0)
-        load_x(1)
-        load_weights([1])
         for axis, f in enumerate((f1, f2, f3)):
             for b in range(BATCH):
-                nc.sync.dma_start(
+                nc.gpsimd.dma_start(
                     out=angles[b:P:BATCH, axis].rearrange("p t c -> p (t c)"),
                     in_=f.rearrange("(m t) c -> m (t c)", t=BATCH * PAIR),
                 )
-        load_weights([2, 3])
-        load_weights([4, 5, 6, 7])
+        load_weights(0)
+        load_x(0)
+        load_x(1)
+        for piece in range(1, len(PIECES) - 1):
+            load_weights(piece)
 
         factors = const.tile([P, BATCH, PAIR, 2, AXES, 2, HALF], F32)
-        warm = const.tile([P, 2], F32)
-        nc.gpsimd.memset(warm[:, 0:1], 0.0)
 
         def make_factors():
             by_token = factors[:].rearrange("p c e z a s i -> p (c e) z a s i")
@@ -119,8 +115,6 @@ def tile_attention_pa_kernel(tc, x, f1, f2, f3, Wqkv, out_0, out_1, out_2):
                 out=by_token[:, :, 1, :, 1, :], in_=halves[:, :, :, 0, :], func=SIN, scale=-1.0
             )
 
-        ident = const.tile([P, P], F32)
-        make_identity(nc, ident[:])
         x_words = [
             x_sb[c][:].bitcast(F32).rearrange("p (e g q u) -> p e g u q", e=PAIR, g=PASSES, u=2)
             for c in range(2)
@@ -144,10 +138,11 @@ def tile_attention_pa_kernel(tc, x, f1, f2, f3, Wqkv, out_0, out_1, out_2):
                         nc.tensor.transpose(
                             turned_words[:, e, u, :], x_words[b][:, e, g, u, :], ident[:]
                         )
-                nc.scalar.copy(
-                    out=x_grouped_words[:, g, b],
-                    in_=turned_words.rearrange("p e u t -> p e t u"),
-                )
+                dst, src = x_grouped_words[:, g, b], turned_words.rearrange("p e u t -> p e t u")
+                if g == 1:
+                    nc.vector.tensor_copy(out=dst, in_=src)
+                else:
+                    nc.scalar.copy(out=dst, in_=src)
 
         def quantise_x(b):
             for g in range(PASSES):
@@ -207,8 +202,8 @@ def tile_attention_pa_kernel(tc, x, f1, f2, f3, Wqkv, out_0, out_1, out_2):
 
         shape = [P, 2, UNIT_HEADS, HEAD_DIM]
 
-        def products(n, scaled):
-            for b in range(BATCH):
+        def products(n, scaled, entries):
+            for b in entries:
                 for e in range(PAIR):
                     nc.vector.tensor_tensor(
                         out=scaled[:, :, :, b, e, :],
@@ -249,61 +244,85 @@ def tile_attention_pa_kernel(tc, x, f1, f2, f3, Wqkv, out_0, out_1, out_2):
                 in_=scaled[b:P:BATCH, 0, :, c].rearrange("p h e d -> p h (e d)"),
             )
 
-        ROWS = BATCH * UNIT_HEADS * PAIR
-        every = slice(0, ROWS)
-        lower = slice(0, ROWS // 2)
-        upper = slice(ROWS // 2, ROWS)
+        every = slice(0, BATCH * UNIT_HEADS * PAIR)
         fence = const.tile([P, 1], U32)
+        scaled_of = {}
+
+        def rotated_result(n):
+            scaled_of[n] = result.tile(
+                [P, 2, UNIT_HEADS, BATCH, PAIR, HEAD_DIM], F32, align_bytes=64, name="scaled"
+            )
+            return scaled_of[n]
+
+        def finish(n):
+            for s in range(2):
+                sums(nc.gpsimd, scaled_of[n], s, every)
+
+        def prepare(n):
+            if n < UNITS:
+                quantise(n)
+                for b in range(BATCH):
+                    multiply(n, b)
+
+        def vector_share(n):
+            if n < 2:
+                return (1, 2)
+            if n < EARLY:
+                return (2,)
+            return () if rotated(order[n - 2]) else (1, 2)
 
         with tc.manual_schedule():
             nc.scalar.activation(out=warm[:, 1:2], in_=warm[:, 0:1], func=SIN)
-            pending = []
-            for n in range(-2, UNITS):
-                if n == -1:
-                    turn_x(0)
-                    quantise_x(0)
-                    turn_x(1)
-                    quantise_x(1)
-                if 0 <= n + 1 < UNITS:
-                    quantise(n + 1)
+            regroup(0, vector_share(0))
+            quantise(0)
+            make_factors()
+            turn_x(0)
+            quantise_x(0)
+            turn_x(1)
+            multiply(0, 0)
+            quantise_x(1)
+            multiply(0, 1)
+            scaled = rotated_result(0)
+            products(0, scaled, (0,))
+            regroup(1, vector_share(1))
+            prepare(1)
+            products(0, scaled, (1,))
+            regroup(2, vector_share(2))
+            finish(0)
+            products(1, rotated_result(1), range(BATCH))
+            for b in range(BATCH):
+                store(0, scaled_of[0], b)
+            prepare(2)
+            regroup(3, vector_share(3))
+            for n in range(2, UNITS):
+                if n == V_TURN:
+                    load_weights(len(PIECES) - 1)
+                prepare(n + 1)
+                if rotated(order[n]):
+                    nc.gpsimd.tensor_copy(out=fence[:], in_=packed_of[n + 1][0][:, 1024:1025])
+                    finish(n - 1)
+                    products(n, rotated_result(n), range(BATCH))
                     for b in range(BATCH):
-                        multiply(n + 1, b)
-                if n >= 0 and rotated(order[n]):
-                    scaled = result.tile(
-                        [P, 2, UNIT_HEADS, BATCH, PAIR, HEAD_DIM], F32, align_bytes=64, name="scaled"
-                    )
-                    if pending:
-                        if n + 1 < UNITS:
-                            nc.gpsimd.tensor_copy(out=fence[:], in_=packed_of[n + 1][0][:, 1024:1025])
-                        sums(nc.gpsimd, pending[1], 0, every)
-                        sums(nc.gpsimd, pending[1], 1, lower)
-                    products(n, scaled)
-                    if pending:
-                        sums(nc.vector, pending[1], 1, upper)
-                        for b in range(BATCH):
-                            store(pending[0], pending[1], b)
-                    pending = [n, scaled]
-                elif n >= 0:
+                        store(n - 1, scaled_of[n - 1], b)
+                else:
                     scaled = result.tile(
                         [P, 1, UNIT_HEADS, BATCH, PAIR, HEAD_DIM], F32, align_bytes=64, name="scaled"
                     )
                     for c in range(2):
                         for e in range(PAIR):
-                            nc.scalar.copy(out=scaled[:, 0, :, c, e, :], in_=banks_of[(n, c, e)])
+                            if n >= UNITS - 2 and e == 1:
+                                nc.vector.tensor_copy(out=scaled[:, 0, :, c, e, :], in_=banks_of[(n, c, e)])
+                            else:
+                                nc.scalar.copy(out=scaled[:, 0, :, c, e, :], in_=banks_of[(n, c, e)])
                         if n == UNITS - 1:
                             for b in range(BATCH):
                                 store_half(n, scaled, b, c)
                     if n < UNITS - 1:
                         for b in range(BATCH):
                             store(n, scaled, b)
-                if n == 2:
-                    load_weights([8, 9, 10, 11])
                 if n + 2 < UNITS:
-                    regroup(n + 2, (1, 2) if n < 0 or not rotated(order[n]) else ())
-                if n == -1:
-                    make_factors()
+                    regroup(n + 2, vector_share(n + 2))
                 if n == ROPE_SECTIONS * UNITS_PER_SECTION - 1:
-                    for s in range(2):
-                        sums(nc.vector, pending[1], s, every)
+                    finish(n)
                     for b in range(BATCH):
-                        store(pending[0], pending[1], b)
+                        store(n, scaled_of[n], b)

@@ -88,7 +88,7 @@ def tile_attention_pa_kernel(tc, x, f1, f2, f3, Wqkv, out_0, out_1, out_2):
 
         for axis, f in enumerate((f1, f2, f3)):
             for b in range(BATCH):
-                nc.gpsimd.dma_start(
+                nc.scalar.dma_start(
                     out=angles[b:P:BATCH, axis].rearrange("p t c -> p (t c)"),
                     in_=f.rearrange("(m t) c -> m (t c)", t=BATCH * PAIR),
                 )
@@ -275,10 +275,10 @@ def tile_attention_pa_kernel(tc, x, f1, f2, f3, Wqkv, out_0, out_1, out_2):
             nc.scalar.activation(out=warm[:, 1:2], in_=warm[:, 0:1], func=SIN)
             regroup(0, vector_share(0))
             quantise(0)
-            make_factors()
             turn_x(0)
             quantise_x(0)
             turn_x(1)
+            make_factors()
             multiply(0, 0)
             quantise_x(1)
             multiply(0, 1)

@@ -244,8 +244,12 @@ def tile_attention_pa_kernel(tc, x, f1, f2, f3, Wqkv, out_0, out_1, out_2):
                 in_=scaled[b:P:BATCH, 0, :, c].rearrange("p h e d -> p h (e d)"),
             )
 
-        every = slice(0, BATCH * UNIT_HEADS * PAIR)
+        ROWS = BATCH * UNIT_HEADS * PAIR
+        every = slice(0, ROWS)
+        lower = slice(0, ROWS // 2)
+        upper = slice(ROWS // 2, ROWS)
         fence = const.tile([P, 1], U32)
+        fence_bf = const.tile([P, 1], BF16)
         scaled_of = {}
 
         def rotated_result(n):
@@ -254,9 +258,12 @@ def tile_attention_pa_kernel(tc, x, f1, f2, f3, Wqkv, out_0, out_1, out_2):
             )
             return scaled_of[n]
 
-        def finish(n):
-            for s in range(2):
-                sums(nc.gpsimd, scaled_of[n], s, every)
+        def gpsimd_sums(n):
+            sums(nc.gpsimd, scaled_of[n], 0, every)
+            sums(nc.gpsimd, scaled_of[n], 1, lower)
+
+        def vector_sums(n):
+            sums(nc.vector, scaled_of[n], 1, upper)
 
         def prepare(n):
             if n < UNITS:
@@ -288,8 +295,13 @@ def tile_attention_pa_kernel(tc, x, f1, f2, f3, Wqkv, out_0, out_1, out_2):
             prepare(1)
             products(0, scaled, (1,))
             regroup(2, vector_share(2))
-            finish(0)
+            nc.gpsimd.tensor_copy(
+                out=fence_bf[:],
+                in_=grouped_of[2][:, PASSES - 1].rearrange("p w j -> p (w j)")[:, PACK * UNIT - 1 :],
+            )
+            gpsimd_sums(0)
             products(1, rotated_result(1), range(BATCH))
+            vector_sums(0)
             for b in range(BATCH):
                 store(0, scaled_of[0], b)
             prepare(2)
@@ -300,8 +312,9 @@ def tile_attention_pa_kernel(tc, x, f1, f2, f3, Wqkv, out_0, out_1, out_2):
                 prepare(n + 1)
                 if rotated(order[n]):
                     nc.gpsimd.tensor_copy(out=fence[:], in_=packed_of[n + 1][0][:, 1024:1025])
-                    finish(n - 1)
+                    gpsimd_sums(n - 1)
                     products(n, rotated_result(n), range(BATCH))
+                    vector_sums(n - 1)
                     for b in range(BATCH):
                         store(n - 1, scaled_of[n - 1], b)
                 else:
@@ -323,6 +336,7 @@ def tile_attention_pa_kernel(tc, x, f1, f2, f3, Wqkv, out_0, out_1, out_2):
                 if n + 2 < UNITS:
                     regroup(n + 2, vector_share(n + 2))
                 if n == ROPE_SECTIONS * UNITS_PER_SECTION - 1:
-                    finish(n)
+                    for s in range(2):
+                        sums(nc.vector, scaled_of[n], s, every)
                     for b in range(BATCH):
                         store(n, scaled_of[n], b)

@@ -31,8 +31,9 @@ UNITS_PER_SECTION = HEADS // UNIT_HEADS
 UNITS = SECTIONS * UNITS_PER_SECTION
 PIECES = ((0,), (1,), (2,), (3, 4), (5, 6, 7), (8, 9, 10, 11))
 V_TURN = 3
-EARLY = 4
 BANK = 512
+PAIR_COLS = 256
+FIRST_PAIRED = 3
 
 FLOPS = 2 * BATCH * TOKENS * DIM * SECTIONS * HEADS * HEAD_DIM
 
@@ -47,7 +48,8 @@ def tile_attention_pa_kernel(tc, x, f1, f2, f3, Wqkv, out_0, out_1, out_2):
         stage = ctx.enter_context(tc.tile_pool(name="stage", bufs=3))
         packed = ctx.enter_context(tc.tile_pool(name="packed", bufs=4))
         result = ctx.enter_context(tc.tile_pool(name="result", bufs=4))
-        psum = ctx.enter_context(tc.psum_pool(name="psum", bufs=8))
+        psum = ctx.enter_context(tc.psum_pool(name="psum", bufs=7))
+        psum_pairs = ctx.enter_context(tc.psum_pool(name="psum_pairs", bufs=1))
 
         order = list(range(UNITS))
 
@@ -85,6 +87,8 @@ def tile_attention_pa_kernel(tc, x, f1, f2, f3, Wqkv, out_0, out_1, out_2):
         nc.gpsimd.memset(warm[:, 0:1], 0.0)
         ident = const.tile([P, P], F32)
         make_identity(nc, ident[:])
+        ident_pairs = const.tile([P, P], BF16)
+        make_identity(nc, ident_pairs[:])
 
         for axis, f in enumerate((f1, f2, f3)):
             for b in range(BATCH):
@@ -155,17 +159,39 @@ def tile_attention_pa_kernel(tc, x, f1, f2, f3, Wqkv, out_0, out_1, out_2):
         grouped_of = {}
         packed_of = {}
 
+        pairs_of = {}
+
+        def pair_up(n):
+            raw, col0 = raw_of[order[n]]
+            bank = psum_pairs.tile([P, PAIR_COLS * PACK], BF16, name="pairs")
+            pairs_of[n] = bank
+            quads = bank[:].rearrange("p (c j) -> p c j", j=PACK)
+            for h in range(2):
+                rows = slice(2 * h, 2 * h + 2)
+                nc.tensor.matmul(
+                    quads[:, :, rows],
+                    lhsT=ident_pairs[:],
+                    rhs=raw[:, 0, rows, col0 : col0 + PAIR_COLS].rearrange("p j c -> p c j"),
+                    start=True,
+                    stop=True,
+                )
+
         def regroup(n, vector_passes):
             raw, col0 = raw_of[order[n]]
             grouped = stage.tile([P, PASSES, UNIT, PACK], BF16, align_bytes=64, name="grouped")
             grouped_of[n] = grouped
             for g in range(PASSES):
-                src = raw[:, g, :, col0 : col0 + UNIT].rearrange("p j (c i) -> p c j i", i=4)
-                dst = grouped[:, g, :, :].rearrange("p (c i) j -> p c j i", i=4)
+                first = PAIR_COLS if g == 0 and n in pairs_of else 0
+                src = raw[:, g, :, col0 + first : col0 + UNIT].rearrange("p j (c i) -> p c j i", i=4)
+                dst = grouped[:, g, first:, :].rearrange("p (c i) j -> p c j i", i=4)
                 if g in vector_passes:
                     nc.vector.tensor_copy(out=dst, in_=src)
                 else:
                     nc.scalar.copy(out=dst, in_=src)
+            if n in pairs_of:
+                nc.scalar.copy(
+                    out=grouped[:, 0, 0:PAIR_COLS, :].rearrange("p c j -> p (c j)"), in_=pairs_of[n][:]
+                )
 
         def quantise(n):
             codes = packed.tile([P, PASSES * UNIT], U32, align_bytes=64, name="codes")
@@ -249,7 +275,6 @@ def tile_attention_pa_kernel(tc, x, f1, f2, f3, Wqkv, out_0, out_1, out_2):
         lower = slice(0, ROWS // 2)
         upper = slice(ROWS // 2, ROWS)
         fence = const.tile([P, 1], U32)
-        fence_bf = const.tile([P, 1], BF16)
         scaled_of = {}
 
         def rotated_result(n):
@@ -274,8 +299,6 @@ def tile_attention_pa_kernel(tc, x, f1, f2, f3, Wqkv, out_0, out_1, out_2):
         def vector_share(n):
             if n < 2:
                 return (1, 2)
-            if n < EARLY:
-                return (2,)
             return () if rotated(order[n - 2]) else (1, 2)
 
         with tc.manual_schedule():
@@ -295,20 +318,11 @@ def tile_attention_pa_kernel(tc, x, f1, f2, f3, Wqkv, out_0, out_1, out_2):
             prepare(1)
             products(0, scaled, (1,))
             regroup(2, vector_share(2))
-            nc.gpsimd.tensor_copy(
-                out=fence_bf[:],
-                in_=grouped_of[2][:, PASSES - 1].rearrange("p w j -> p (w j)")[:, PACK * UNIT - 1 :],
-            )
-            gpsimd_sums(0)
-            products(1, rotated_result(1), range(BATCH))
-            vector_sums(0)
-            for b in range(BATCH):
-                store(0, scaled_of[0], b)
-            prepare(2)
-            regroup(3, vector_share(3))
-            for n in range(2, UNITS):
+            for n in range(1, UNITS):
                 if n == V_TURN:
                     load_weights(len(PIECES) - 1)
+                if FIRST_PAIRED <= n + 2 < UNITS:
+                    pair_up(n + 2)
                 prepare(n + 1)
                 if rotated(order[n]):
                     nc.gpsimd.tensor_copy(out=fence[:], in_=packed_of[n + 1][0][:, 1024:1025])
@@ -323,7 +337,7 @@ def tile_attention_pa_kernel(tc, x, f1, f2, f3, Wqkv, out_0, out_1, out_2):
                     )
                     for c in range(2):
                         for e in range(PAIR):
-                            if n >= UNITS - 2 and e == 1:
+                            if n == UNITS - 1 and e == 1:
                                 nc.vector.tensor_copy(out=scaled[:, 0, :, c, e, :], in_=banks_of[(n, c, e)])
                             else:
                                 nc.scalar.copy(out=scaled[:, 0, :, c, e, :], in_=banks_of[(n, c, e)])

@@ -30,10 +30,12 @@ WIDE = 256
 UNITS_PER_SECTION = HEADS // UNIT_HEADS
 UNITS = SECTIONS * UNITS_PER_SECTION
 PIECES = ((0,), (1,), (2,), (3, 4), (5, 6, 7), (8, 9, 10, 11))
-V_TURN = 3
-BANK = 512
+V_TURN = 2
+PAIR_BANKS = 2
 PAIR_COLS = 256
-FIRST_PAIRED = 3
+PAIR_PASSES = (0, 1)
+FIRST_PAIRED = 4
+BANK = 512
 
 FLOPS = 2 * BATCH * TOKENS * DIM * SECTIONS * HEADS * HEAD_DIM
 
@@ -47,9 +49,9 @@ def tile_attention_pa_kernel(tc, x, f1, f2, f3, Wqkv, out_0, out_1, out_2):
         fetched = ctx.enter_context(tc.tile_pool(name="fetched", bufs=1))
         stage = ctx.enter_context(tc.tile_pool(name="stage", bufs=3))
         packed = ctx.enter_context(tc.tile_pool(name="packed", bufs=4))
-        result = ctx.enter_context(tc.tile_pool(name="result", bufs=4))
-        psum = ctx.enter_context(tc.psum_pool(name="psum", bufs=7))
-        psum_pairs = ctx.enter_context(tc.psum_pool(name="psum_pairs", bufs=1))
+        result = ctx.enter_context(tc.tile_pool(name="result", bufs=5))
+        psum = ctx.enter_context(tc.psum_pool(name="psum", bufs=8 - PAIR_BANKS))
+        psum_pairs = ctx.enter_context(tc.psum_pool(name="psum_pairs", bufs=PAIR_BANKS))
 
         order = list(range(UNITS))
 
@@ -96,9 +98,9 @@ def tile_attention_pa_kernel(tc, x, f1, f2, f3, Wqkv, out_0, out_1, out_2):
                     out=angles[b:P:BATCH, axis].rearrange("p t c -> p (t c)"),
                     in_=f.rearrange("(m t) c -> m (t c)", t=BATCH * PAIR),
                 )
-        load_weights(0)
         load_x(0)
         load_x(1)
+        load_weights(0)
         for piece in range(1, len(PIECES) - 1):
             load_weights(piece)
 
@@ -163,46 +165,52 @@ def tile_attention_pa_kernel(tc, x, f1, f2, f3, Wqkv, out_0, out_1, out_2):
 
         def pair_up(n):
             raw, col0 = raw_of[order[n]]
-            bank = psum_pairs.tile([P, PAIR_COLS * PACK], BF16, name="pairs")
-            pairs_of[n] = bank
-            quads = bank[:].rearrange("p (c j) -> p c j", j=PACK)
-            for h in range(2):
-                rows = slice(2 * h, 2 * h + 2)
-                nc.tensor.matmul(
-                    quads[:, :, rows],
-                    lhsT=ident_pairs[:],
-                    rhs=raw[:, 0, rows, col0 : col0 + PAIR_COLS].rearrange("p j c -> p c j"),
-                    start=True,
-                    stop=True,
-                )
+            for g in PAIR_PASSES:
+                bank = psum_pairs.tile([P, PAIR_COLS * PACK], BF16, name="pairs")
+                pairs_of[(n, g)] = bank
+                quads = bank[:].rearrange("p (c j) -> p c j", j=PACK)
+                for h in range(2):
+                    rows = slice(2 * h, 2 * h + 2)
+                    nc.tensor.matmul(
+                        quads[:, :, rows],
+                        lhsT=ident_pairs[:],
+                        rhs=raw[:, g, rows, col0 : col0 + PAIR_COLS].rearrange("p j c -> p c j"),
+                        start=True,
+                        stop=True,
+                    )
 
         def regroup(n, vector_passes):
             raw, col0 = raw_of[order[n]]
             grouped = stage.tile([P, PASSES, UNIT, PACK], BF16, align_bytes=64, name="grouped")
             grouped_of[n] = grouped
             for g in range(PASSES):
-                first = PAIR_COLS if g == 0 and n in pairs_of else 0
+                first = PAIR_COLS if (n, g) in pairs_of else 0
                 src = raw[:, g, :, col0 + first : col0 + UNIT].rearrange("p j (c i) -> p c j i", i=4)
                 dst = grouped[:, g, first:, :].rearrange("p (c i) j -> p c j i", i=4)
                 if g in vector_passes:
                     nc.vector.tensor_copy(out=dst, in_=src)
                 else:
                     nc.scalar.copy(out=dst, in_=src)
-            if n in pairs_of:
-                nc.scalar.copy(
-                    out=grouped[:, 0, 0:PAIR_COLS, :].rearrange("p c j -> p (c j)"), in_=pairs_of[n][:]
-                )
+            for g in PAIR_PASSES:
+                if (n, g) in pairs_of:
+                    nc.scalar.copy(
+                        out=grouped[:, g, 0:PAIR_COLS, :].rearrange("p c j -> p (c j)"),
+                        in_=pairs_of[(n, g)][:],
+                    )
 
-        def quantise(n):
-            codes = packed.tile([P, PASSES * UNIT], U32, align_bytes=64, name="codes")
-            scales = packed.tile([P, PASSES * UNIT], U8, align_bytes=64, name="scales")
-            packed_of[n] = (codes, scales)
+        def quantise(n, parts):
+            if n not in packed_of:
+                packed_of[n] = (
+                    packed.tile([P, PASSES * UNIT], U32, align_bytes=64, name="codes"),
+                    packed.tile([P, PASSES * UNIT], U8, align_bytes=64, name="scales"),
+                )
+            codes, scales = packed_of[n]
             flat = grouped_of[n][:].rearrange("p g w j -> p (g w j)")
-            for part in (slice(0, 1024), slice(1024, PASSES * UNIT)):
+            for a, z in parts:
                 nc.vector.quantize_mx(
-                    out=codes[:, part].bitcast(FP8X4),
-                    scales=scales[:, part],
-                    in_=flat[:, PACK * part.start : PACK * part.stop],
+                    out=codes[:, a:z].bitcast(FP8X4),
+                    scales=scales[:, a:z],
+                    in_=flat[:, PACK * a : PACK * z],
                 )
 
         banks_of = {}
@@ -290,39 +298,57 @@ def tile_attention_pa_kernel(tc, x, f1, f2, f3, Wqkv, out_0, out_1, out_2):
         def vector_sums(n):
             sums(nc.vector, scaled_of[n], 1, upper)
 
+        WHOLE = ((0, 1024), (1024, 1152))
+        BY_PASS = ((0, 512), (512, 768), (768, 1024), (1024, 1152))
+
         def prepare(n):
             if n < UNITS:
-                quantise(n)
+                quantise(n, WHOLE)
                 for b in range(BATCH):
                     multiply(n, b)
 
-        def vector_share(n):
-            if n < 2:
-                return (1, 2)
-            return () if rotated(order[n - 2]) else (1, 2)
+        def emit(n):
+            scaled = result.tile(
+                [P, 1, UNIT_HEADS, BATCH, PAIR, HEAD_DIM], F32, align_bytes=64, name="scaled"
+            )
+            for c in range(2):
+                for e in range(PAIR):
+                    if n == UNITS - 3 or (n == UNITS - 1 and e == 1):
+                        nc.vector.tensor_copy(out=scaled[:, 0, :, c, e, :], in_=banks_of[(n, c, e)])
+                    else:
+                        nc.scalar.copy(out=scaled[:, 0, :, c, e, :], in_=banks_of[(n, c, e)])
+                if n == UNITS - 1:
+                    for b in range(BATCH):
+                        store_half(n, scaled, b, c)
+            if n < UNITS - 1:
+                for b in range(BATCH):
+                    store(n, scaled, b)
+
+        last_rotated = ROPE_SECTIONS * UNITS_PER_SECTION - 1
 
         with tc.manual_schedule():
             nc.scalar.activation(out=warm[:, 1:2], in_=warm[:, 0:1], func=SIN)
-            regroup(0, vector_share(0))
-            quantise(0)
-            turn_x(0)
-            quantise_x(0)
-            turn_x(1)
+            for b in range(BATCH):
+                turn_x(b)
+                quantise_x(b)
+            regroup(0, (1, 2))
+            quantise(0, BY_PASS)
             make_factors()
-            multiply(0, 0)
-            quantise_x(1)
-            multiply(0, 1)
-            scaled = rotated_result(0)
-            products(0, scaled, (0,))
-            regroup(1, vector_share(1))
+            for b in range(BATCH):
+                multiply(0, b)
+            products(0, rotated_result(0), range(BATCH))
+            regroup(1, (2,))
             prepare(1)
-            products(0, scaled, (1,))
-            regroup(2, vector_share(2))
+            regroup(2, (2,))
             for n in range(1, UNITS):
                 if n == V_TURN:
                     load_weights(len(PIECES) - 1)
-                if FIRST_PAIRED <= n + 2 < UNITS:
-                    pair_up(n + 2)
+                if n == 2:
+                    pair_up(4)
+                    regroup(4, ())
+                ahead = n + 2 if n < 2 else n + 3
+                if FIRST_PAIRED <= ahead < UNITS:
+                    pair_up(ahead)
                 prepare(n + 1)
                 if rotated(order[n]):
                     nc.gpsimd.tensor_copy(out=fence[:], in_=packed_of[n + 1][0][:, 1024:1025])
@@ -332,25 +358,11 @@ def tile_attention_pa_kernel(tc, x, f1, f2, f3, Wqkv, out_0, out_1, out_2):
                     for b in range(BATCH):
                         store(n - 1, scaled_of[n - 1], b)
                 else:
-                    scaled = result.tile(
-                        [P, 1, UNIT_HEADS, BATCH, PAIR, HEAD_DIM], F32, align_bytes=64, name="scaled"
-                    )
-                    for c in range(2):
-                        for e in range(PAIR):
-                            if n == UNITS - 1 and e == 1:
-                                nc.vector.tensor_copy(out=scaled[:, 0, :, c, e, :], in_=banks_of[(n, c, e)])
-                            else:
-                                nc.scalar.copy(out=scaled[:, 0, :, c, e, :], in_=banks_of[(n, c, e)])
-                        if n == UNITS - 1:
-                            for b in range(BATCH):
-                                store_half(n, scaled, b, c)
-                    if n < UNITS - 1:
+                    if n == last_rotated + 1:
+                        for s in range(2):
+                            sums(nc.vector, scaled_of[last_rotated], s, every)
                         for b in range(BATCH):
-                            store(n, scaled, b)
-                if n + 2 < UNITS:
-                    regroup(n + 2, vector_share(n + 2))
-                if n == ROPE_SECTIONS * UNITS_PER_SECTION - 1:
-                    for s in range(2):
-                        sums(nc.vector, scaled_of[n], s, every)
-                    for b in range(BATCH):
-                        store(n, scaled_of[n], b)
+                            store(last_rotated, scaled_of[last_rotated], b)
+                    emit(n)
+                if ahead < UNITS:
+                    regroup(ahead, ())

@@ -179,7 +179,7 @@ def tile_attention_pa_kernel(tc, x, f1, f2, f3, Wqkv, out_0, out_1, out_2):
                         stop=True,
                     )
 
-        def regroup(n, vector_passes):
+        def regroup(n, vector_passes, gpsimd_passes=()):
             raw, col0 = raw_of[order[n]]
             grouped = stage.tile([P, PASSES, UNIT, PACK], BF16, align_bytes=64, name="grouped")
             grouped_of[n] = grouped
@@ -189,6 +189,10 @@ def tile_attention_pa_kernel(tc, x, f1, f2, f3, Wqkv, out_0, out_1, out_2):
                 dst = grouped[:, g, first:, :].rearrange("p (c i) j -> p c j i", i=4)
                 if g in vector_passes:
                     nc.vector.tensor_copy(out=dst, in_=src)
+                elif g in gpsimd_passes:
+                    nc.gpsimd.tensor_scalar(
+                        out=dst, in0=src, scalar1=1.0, scalar2=0.0, op0=MULT, op1=ADD
+                    )
                 else:
                     nc.scalar.copy(out=dst, in_=src)
             for g in PAIR_PASSES:
@@ -337,7 +341,8 @@ def tile_attention_pa_kernel(tc, x, f1, f2, f3, Wqkv, out_0, out_1, out_2):
             for b in range(BATCH):
                 multiply(0, b)
             products(0, rotated_result(0), range(BATCH))
-            regroup(1, (2,))
+            nc.gpsimd.tensor_copy(out=fence[:], in_=packed_of[0][0][:, 1151:1152])
+            regroup(1, (), (1,))
             prepare(1)
             regroup(2, (2,))
             for n in range(1, UNITS):
@@ -363,6 +368,9 @@ def tile_attention_pa_kernel(tc, x, f1, f2, f3, Wqkv, out_0, out_1, out_2):
                             sums(nc.vector, scaled_of[last_rotated], s, every)
                         for b in range(BATCH):
                             store(last_rotated, scaled_of[last_rotated], b)
-                    emit(n)
+                    if n > last_rotated + 1:
+                        emit(n)
                 if ahead < UNITS:
                     regroup(ahead, ())
+                if n == last_rotated:
+                    emit(n + 1)

@@ -35,6 +35,7 @@ PAIR_BANKS = 2
 PAIR_COLS = 256
 PAIR_PASSES = (0, 1)
 FIRST_PAIRED = 4
+RUN = 8
 BANK = 512
 
 FLOPS = 2 * BATCH * TOKENS * DIM * SECTIONS * HEADS * HEAD_DIM
@@ -185,8 +186,8 @@ def tile_attention_pa_kernel(tc, x, f1, f2, f3, Wqkv, out_0, out_1, out_2):
             grouped_of[n] = grouped
             for g in range(PASSES):
                 first = PAIR_COLS if (n, g) in pairs_of else 0
-                src = raw[:, g, :, col0 + first : col0 + UNIT].rearrange("p j (c i) -> p c j i", i=4)
-                dst = grouped[:, g, first:, :].rearrange("p (c i) j -> p c j i", i=4)
+                src = raw[:, g, :, col0 + first : col0 + UNIT].rearrange("p j (c i) -> p c j i", i=RUN)
+                dst = grouped[:, g, first:, :].rearrange("p (c i) j -> p c j i", i=RUN)
                 if g in vector_passes:
                     nc.vector.tensor_copy(out=dst, in_=src)
                 elif g in gpsimd_passes:

@@ -38,6 +38,10 @@ FIRST_PAIRED = 4
 RUN = 8
 BANK = 512
 
+U0 = ((0, 0, 384, "scalar"), (1, 0, 384, "vector"), (2, 0, 384, "vector"))
+U1 = ((0, 0, 384, "scalar"), (1, 0, 384, "gpsimd"), (2, 0, 384, "scalar"))
+U2 = ((0, 0, 192, "gpsimd"), (0, 192, 384, "scalar"), (1, 0, 384, "scalar"), (2, 0, 192, "vector"), (2, 192, 384, "scalar"))
+
 FLOPS = 2 * BATCH * TOKENS * DIM * SECTIONS * HEADS * HEAD_DIM
 
 
@@ -180,22 +184,26 @@ def tile_attention_pa_kernel(tc, x, f1, f2, f3, Wqkv, out_0, out_1, out_2):
                         stop=True,
                     )
 
-        def regroup(n, vector_passes, gpsimd_passes=()):
+        def regroup(n, shares=None):
             raw, col0 = raw_of[order[n]]
             grouped = stage.tile([P, PASSES, UNIT, PACK], BF16, align_bytes=64, name="grouped")
             grouped_of[n] = grouped
-            for g in range(PASSES):
-                first = PAIR_COLS if (n, g) in pairs_of else 0
-                src = raw[:, g, :, col0 + first : col0 + UNIT].rearrange("p j (c i) -> p c j i", i=RUN)
-                dst = grouped[:, g, first:, :].rearrange("p (c i) j -> p c j i", i=RUN)
-                if g in vector_passes:
+            if shares is None:
+                shares = [
+                    (g, PAIR_COLS if (n, g) in pairs_of else 0, UNIT, "scalar")
+                    for g in range(PASSES)
+                ]
+            for g, a, z, engine in shares:
+                src = raw[:, g, :, col0 + a : col0 + z].rearrange("p j (c i) -> p c j i", i=RUN)
+                dst = grouped[:, g, a:z, :].rearrange("p (c i) j -> p c j i", i=RUN)
+                if engine == "vector":
                     nc.vector.tensor_copy(out=dst, in_=src)
-                elif g in gpsimd_passes:
+                elif engine == "scalar":
+                    nc.scalar.copy(out=dst, in_=src)
+                else:
                     nc.gpsimd.tensor_scalar(
                         out=dst, in0=src, scalar1=1.0, scalar2=0.0, op0=MULT, op1=ADD
                     )
-                else:
-                    nc.scalar.copy(out=dst, in_=src)
             for g in PAIR_PASSES:
                 if (n, g) in pairs_of:
                     nc.scalar.copy(
@@ -336,22 +344,22 @@ def tile_attention_pa_kernel(tc, x, f1, f2, f3, Wqkv, out_0, out_1, out_2):
             for b in range(BATCH):
                 turn_x(b)
                 quantise_x(b)
-            regroup(0, (1, 2))
+            regroup(0, U0)
             quantise(0, BY_PASS)
             make_factors()
             for b in range(BATCH):
                 multiply(0, b)
             products(0, rotated_result(0), range(BATCH))
             nc.gpsimd.tensor_copy(out=fence[:], in_=packed_of[0][0][:, 1151:1152])
-            regroup(1, (), (1,))
+            regroup(1, U1)
             prepare(1)
-            regroup(2, (2,))
+            regroup(2, U2)
             for n in range(1, UNITS):
                 if n == V_TURN:
                     load_weights(len(PIECES) - 1)
                 if n == 2:
                     pair_up(4)
-                    regroup(4, ())
+                    regroup(4)
                 ahead = n + 2 if n < 2 else n + 3
                 if FIRST_PAIRED <= ahead < UNITS:
                     pair_up(ahead)
@@ -372,6 +380,6 @@ def tile_attention_pa_kernel(tc, x, f1, f2, f3, Wqkv, out_0, out_1, out_2):
                     if n > last_rotated + 1:
                         emit(n)
                 if ahead < UNITS:
-                    regroup(ahead, ())
+                    regroup(ahead)
                 if n == last_rotated:
                     emit(n + 1)

import math
from contextlib import ExitStack

import concourse.mybir as mybir
from concourse.masks import make_identity

F32 = mybir.dt.float32
BF16 = mybir.dt.bfloat16
U32 = mybir.dt.uint32
U8 = mybir.dt.uint8
FP8X4 = mybir.dt.float8_e4m3fn_x4
MULT = mybir.AluOpType.mult
ADD = mybir.AluOpType.add
SIN = mybir.ActivationFunctionType.Sin

BATCH, TOKENS, DIM, HEADS, HEAD_DIM = 2, 256, 1536, 16, 96
SECTIONS = 3
ROPE_SECTIONS = 2
AXES, HALF = 3, 16

P = 128
PACK = 4
K_PASS = P * PACK
PASSES = DIM // K_PASS
PAIR = TOKENS // P

UNIT_HEADS = 4
UNIT = UNIT_HEADS * HEAD_DIM
WIDE = 256
UNITS_PER_SECTION = HEADS // UNIT_HEADS
UNITS = SECTIONS * UNITS_PER_SECTION
PIECES = ((0,), (1,), (2,), (3, 4), (5, 6, 7), (8, 9, 10, 11))
V_TURN = 2
PAIR_BANKS = 2
PAIR_COLS = 256
PAIR_PASSES = (0, 1)
FIRST_PAIRED = 4
RUN = 8
BANK = 512

U0 = ((0, 0, 384, "scalar"), (1, 0, 384, "vector"), (2, 0, 384, "vector"))
U1 = ((0, 0, 384, "scalar"), (1, 0, 384, "gpsimd"), (2, 0, 384, "scalar"))
U2 = ((0, 0, 192, "gpsimd"), (0, 192, 384, "scalar"), (1, 0, 384, "scalar"), (2, 0, 192, "vector"), (2, 192, 384, "scalar"))

FLOPS = 2 * BATCH * TOKENS * DIM * SECTIONS * HEADS * HEAD_DIM


def tile_attention_pa_kernel(tc, x, f1, f2, f3, Wqkv, out_0, out_1, out_2):
    nc = tc.nc
    outs = (out_0, out_1, out_2)

    with ExitStack() as ctx:
        const = ctx.enter_context(tc.tile_pool(name="const", bufs=1))
        fetched = ctx.enter_context(tc.tile_pool(name="fetched", bufs=1))
        stage = ctx.enter_context(tc.tile_pool(name="stage", bufs=3))
        packed = ctx.enter_context(tc.tile_pool(name="packed", bufs=4))
        result = ctx.enter_context(tc.tile_pool(name="result", bufs=5))
        psum = ctx.enter_context(tc.psum_pool(name="psum", bufs=8 - PAIR_BANKS))
        psum_pairs = ctx.enter_context(tc.psum_pool(name="psum_pairs", bufs=PAIR_BANKS))

        order = list(range(UNITS))

        def rotated(unit):
            return unit // UNITS_PER_SECTION < ROPE_SECTIONS

        x_sb = [
            result.tile([P, PAIR * DIM], BF16, align_bytes=64, name="scaled") for c in range(2)
        ]
        raw_of = {}

        def load_x(c):
            for b in range(BATCH):
                nc.sync.dma_start(
                    out=x_sb[c][b:P:BATCH, :],
                    in_=x[b].rearrange("(m c f) k -> m c (f k)", c=2, f=PAIR)[:, c, :],
                )

        def load_weights(piece):
            cols = len(PIECES[piece]) * UNIT
            col0 = PIECES[piece][0] * UNIT
            w_raw = fetched.tile([P, PASSES, PACK, cols], BF16, name="w_raw%d" % piece)
            for g in range(PASSES):
                nc.sync.dma_start(
                    out=w_raw[:, g, :, :],
                    in_=Wqkv[g * K_PASS : (g + 1) * K_PASS, col0 : col0 + cols].rearrange(
                        "(p j) w -> p j w", j=PACK
                    ),
                )
            for i, unit in enumerate(PIECES[piece]):
                raw_of[unit] = (w_raw, i * UNIT)

        angles = const.tile([P, AXES, BATCH * PAIR, 2 * HALF], BF16)
        warm = const.tile([P, 2], F32)
        nc.gpsimd.memset(warm[:, 0:1], 0.0)
        ident = const.tile([P, P], F32)
        make_identity(nc, ident[:])
        ident_pairs = const.tile([P, P], BF16)
        make_identity(nc, ident_pairs[:])

        for axis, f in enumerate((f1, f2, f3)):
            for b in range(BATCH):
                nc.scalar.dma_start(
                    out=angles[b:P:BATCH, axis].rearrange("p t c -> p (t c)"),
                    in_=f.rearrange("(m t) c -> m (t c)", t=BATCH * PAIR),
                )
        load_x(0)
        load_x(1)
        load_weights(0)
        for piece in range(1, len(PIECES) - 1):
            load_weights(piece)

        factors = const.tile([P, BATCH, PAIR, 2, AXES, 2, HALF], F32)

        def make_factors():
            by_token = factors[:].rearrange("p c e z a s i -> p (c e) z a s i")
            halves = angles[:].rearrange("p a t (s i) -> p t a s i", s=2)
            nc.scalar.activation(
                out=by_token[:, :, 0].rearrange("p t a s i -> p t a (s i)"),
                in_=angles[:].rearrange("p a t c -> p t a c"),
                func=SIN,
                scale=-1.0,
                bias=math.pi / 2,
            )
            nc.scalar.activation(out=by_token[:, :, 1, :, 0, :], in_=halves[:, :, :, 1, :], func=SIN)
            nc.scalar.activation(
                out=by_token[:, :, 1, :, 1, :], in_=halves[:, :, :, 0, :], func=SIN, scale=-1.0
            )

        x_words = [
            x_sb[c][:].bitcast(F32).rearrange("p (e g q u) -> p e g u q", e=PAIR, g=PASSES, u=2)
            for c in range(2)
        ]
        x_grouped = result.tile(
            [P, PASSES * BATCH * PAIR * P * PACK], BF16, align_bytes=64, name="scaled"
        )
        x_grouped_words = x_grouped[:].bitcast(F32).rearrange(
            "p (g b e t u) -> p g b e t u", g=PASSES, b=BATCH, e=PAIR, u=2
        )
        x_grouped_cols = x_grouped[:].rearrange("p (g b c) -> p g b c", g=PASSES, b=BATCH)
        x_codes = const.tile([P, PASSES, BATCH, PAIR * P], U32, align_bytes=64)
        x_scales = const.tile([P, PASSES, BATCH, PAIR * P], U8, align_bytes=64)

        def turn_x(b):
            for g in range(PASSES):
                turned = psum.tile([P, BANK], F32, name="bank")
                turned_words = turned[:].rearrange("p (e u t) -> p e u t", e=PAIR, u=2)
                for e in range(PAIR):
                    for u in range(2):
                        nc.tensor.transpose(
                            turned_words[:, e, u, :], x_words[b][:, e, g, u, :], ident[:]
                        )
                dst, src = x_grouped_words[:, g, b], turned_words.rearrange("p e u t -> p e t u")
                if g == 1:
                    nc.vector.tensor_copy(out=dst, in_=src)
                else:
                    nc.scalar.copy(out=dst, in_=src)

        def quantise_x(b):
            for g in range(PASSES):
                nc.vector.quantize_mx(
                    out=x_codes[:, g, b, :].bitcast(FP8X4),
                    scales=x_scales[:, g, b, :],
                    in_=x_grouped_cols[:, g, b, :],
                )

        grouped_of = {}
        packed_of = {}

        pairs_of = {}

        def pair_up(n):
            raw, col0 = raw_of[order[n]]
            for g in PAIR_PASSES:
                bank = psum_pairs.tile([P, PAIR_COLS * PACK], BF16, name="pairs")
                pairs_of[(n, g)] = bank
                quads = bank[:].rearrange("p (c j) -> p c j", j=PACK)
                for h in range(2):
                    rows = slice(2 * h, 2 * h + 2)
                    nc.tensor.matmul(
                        quads[:, :, rows],
                        lhsT=ident_pairs[:],
                        rhs=raw[:, g, rows, col0 : col0 + PAIR_COLS].rearrange("p j c -> p c j"),
                        start=True,
                        stop=True,
                    )

        def regroup(n, shares=None):
            raw, col0 = raw_of[order[n]]
            grouped = stage.tile([P, PASSES, UNIT, PACK], BF16, align_bytes=64, name="grouped")
            grouped_of[n] = grouped
            if shares is None:
                shares = [
                    (g, PAIR_COLS if (n, g) in pairs_of else 0, UNIT, "scalar")
                    for g in range(PASSES)
                ]
            for g, a, z, engine in shares:
                src = raw[:, g, :, col0 + a : col0 + z].rearrange("p j (c i) -> p c j i", i=RUN)
                dst = grouped[:, g, a:z, :].rearrange("p (c i) j -> p c j i", i=RUN)
                if engine == "vector":
                    nc.vector.tensor_copy(out=dst, in_=src)
                elif engine == "scalar":
                    nc.scalar.copy(out=dst, in_=src)
                else:
                    nc.gpsimd.tensor_scalar(
                        out=dst, in0=src, scalar1=1.0, scalar2=0.0, op0=MULT, op1=ADD
                    )
            for g in PAIR_PASSES:
                if (n, g) in pairs_of:
                    nc.scalar.copy(
                        out=grouped[:, g, 0:PAIR_COLS, :].rearrange("p c j -> p (c j)"),
                        in_=pairs_of[(n, g)][:],
                    )

        def quantise(n, parts):
            if n not in packed_of:
                packed_of[n] = (
                    packed.tile([P, PASSES * UNIT], U32, align_bytes=64, name="codes"),
                    packed.tile([P, PASSES * UNIT], U8, align_bytes=64, name="scales"),
                )
            codes, scales = packed_of[n]
            flat = grouped_of[n][:].rearrange("p g w j -> p (g w j)")
            for a, z in parts:
                nc.vector.quantize_mx(
                    out=codes[:, a:z].bitcast(FP8X4),
                    scales=scales[:, a:z],
                    in_=flat[:, PACK * a : PACK * z],
                )

        banks_of = {}

        def multiply(n, b):
            codes, scales = packed_of[n]
            for e in range(PAIR):
                bank = psum.tile([P, BANK], F32, name="bank")
                tokens = slice(e * P, (e + 1) * P)
                for part in (slice(0, WIDE), slice(WIDE, UNIT)):
                    for g in range(PASSES):
                        cols = slice(g * UNIT + part.start, g * UNIT + part.stop)
                        nc.tensor.matmul_mx(
                            out=bank[:, part],
                            lhsT=x_codes[:, g, b, tokens].bitcast(FP8X4),
                            lhsT_scale=x_scales[:, g, b, tokens],
                            rhs=codes[:, cols].bitcast(FP8X4),
                            rhs_scale=scales[:, cols],
                            start=(g == 0),
                            stop=(g == PASSES - 1),
                        )
                banks_of[(n, b, e)] = bank[:, 0:UNIT].rearrange("p (h d) -> p h d", h=UNIT_HEADS)

        shape = [P, 2, UNIT_HEADS, HEAD_DIM]

        def products(n, scaled, entries):
            for b in entries:
                for e in range(PAIR):
                    nc.vector.tensor_tensor(
                        out=scaled[:, :, :, b, e, :],
                        in0=banks_of[(n, b, e)].unsqueeze(1).to_broadcast(shape),
                        in1=factors[:, b, e]
                        .rearrange("p z a s i -> p z (a s i)")
                        .unsqueeze(2)
                        .to_broadcast(shape),
                        op=MULT,
                    )

        def sums(engine, scaled, s, rows):
            halves = scaled[:].rearrange("p z h c e (a s i) -> p z (h c e) a s i", a=AXES, s=2)
            engine.tensor_tensor(
                out=halves[:, 0, rows, :, s, :],
                in0=halves[:, 0, rows, :, s, :],
                in1=halves[:, 1, rows, :, 1 - s, :],
                op=ADD,
            )

        def store(n, scaled, b):
            unit = order[n]
            head = (unit % UNITS_PER_SECTION) * UNIT_HEADS
            nc.sync.dma_start(
                out=outs[unit // UNITS_PER_SECTION][b, head : head + UNIT_HEADS].rearrange(
                    "h (m t) d -> m h (t d)", t=BATCH * PAIR
                ),
                in_=scaled[b:P:BATCH, 0].rearrange("p h c e d -> p h (c e d)"),
            )

        def store_half(n, scaled, b, c):
            unit = order[n]
            head = (unit % UNITS_PER_SECTION) * UNIT_HEADS
            nc.sync.dma_start(
                out=outs[unit // UNITS_PER_SECTION][b, head : head + UNIT_HEADS].rearrange(
                    "h (m c f) d -> m h c (f d)", c=2, f=PAIR
                )[:, :, c, :],
                in_=scaled[b:P:BATCH, 0, :, c].rearrange("p h e d -> p h (e d)"),
            )

        ROWS = BATCH * UNIT_HEADS * PAIR
        every = slice(0, ROWS)
        lower = slice(0, ROWS // 2)
        upper = slice(ROWS // 2, ROWS)
        fence = const.tile([P, 1], U32)
        scaled_of = {}

        def rotated_result(n):
            scaled_of[n] = result.tile(
                [P, 2, UNIT_HEADS, BATCH, PAIR, HEAD_DIM], F32, align_bytes=64, name="scaled"
            )
            return scaled_of[n]

        def gpsimd_sums(n):
            sums(nc.gpsimd, scaled_of[n], 0, every)
            sums(nc.gpsimd, scaled_of[n], 1, lower)

        def vector_sums(n):
            sums(nc.vector, scaled_of[n], 1, upper)

        WHOLE = ((0, 1024), (1024, 1152))
        BY_PASS = ((0, 512), (512, 768), (768, 1024), (1024, 1152))

        def prepare(n):
            if n < UNITS:
                quantise(n, WHOLE)
                for b in range(BATCH):
                    multiply(n, b)

        def emit(n):
            scaled = result.tile(
                [P, 1, UNIT_HEADS, BATCH, PAIR, HEAD_DIM], F32, align_bytes=64, name="scaled"
            )
            for c in range(2):
                for e in range(PAIR):
                    if n == UNITS - 3 or (n == UNITS - 1 and e == 1):
                        nc.vector.tensor_copy(out=scaled[:, 0, :, c, e, :], in_=banks_of[(n, c, e)])
                    else:
                        nc.scalar.copy(out=scaled[:, 0, :, c, e, :], in_=banks_of[(n, c, e)])
                if n == UNITS - 1:
                    for b in range(BATCH):
                        store_half(n, scaled, b, c)
            if n < UNITS - 1:
                for b in range(BATCH):
                    store(n, scaled, b)

        last_rotated = ROPE_SECTIONS * UNITS_PER_SECTION - 1

        with tc.manual_schedule():
            nc.scalar.activation(out=warm[:, 1:2], in_=warm[:, 0:1], func=SIN)
            for b in range(BATCH):
                turn_x(b)
                quantise_x(b)
            regroup(0, U0)
            quantise(0, BY_PASS)
            make_factors()
            for b in range(BATCH):
                multiply(0, b)
            products(0, rotated_result(0), range(BATCH))
            nc.gpsimd.tensor_copy(out=fence[:], in_=packed_of[0][0][:, 1151:1152])
            regroup(1, U1)
            prepare(1)
            regroup(2, U2)
            for n in range(1, UNITS):
                if n == V_TURN:
                    load_weights(len(PIECES) - 1)
                if n == 2:
                    pair_up(4)
                    regroup(4)
                ahead = n + 2 if n < 2 else n + 3
                if FIRST_PAIRED <= ahead < UNITS:
                    pair_up(ahead)
                prepare(n + 1)
                if rotated(order[n]):
                    nc.gpsimd.tensor_copy(out=fence[:], in_=packed_of[n + 1][0][:, 1024:1025])
                    gpsimd_sums(n - 1)
                    products(n, rotated_result(n), range(BATCH))
                    vector_sums(n - 1)
                    for b in range(BATCH):
                        store(n - 1, scaled_of[n - 1], b)
                else:
                    if n == last_rotated + 1:
                        for s in range(2):
                            sums(nc.vector, scaled_of[last_rotated], s, every)
                        for b in range(BATCH):
                            store(last_rotated, scaled_of[last_rotated], b)
                    if n > last_rotated + 1:
                        emit(n)
                if ahead < UNITS:
                    regroup(ahead)
                if n == last_rotated:
                    emit(n + 1)
